import numpy as np
import ml_dtypes

BF16 = ml_dtypes.bfloat16


def bf(x):
    return np.asarray(x, np.float32).astype(BF16)


def f32(x):
    return np.asarray(x, np.float32)


def f64(x):
    return np.asarray(x).astype(np.float64)


def striped(idx):
    return np.tile(idx.reshape(-1, 16).T, (8, 1))


B, C, S, K, M, N, H = 2, 512, 1024, 4, 512, 8192, 512


def setup_inputs():
    idx = np.concatenate([np.random.permutation(S)[:H] for _ in range(N // H)])
    return {"x": f32(np.random.standard_normal((B, C, S))), "wc": bf(np.random.standard_normal((C, M)) / np.sqrt(2.0 * C)), "wd": bf(np.random.standard_normal((C, M)) / np.sqrt(2.0 * C)), "bias": f32(0.1 * np.random.standard_normal((M, 1))), "offs": striped(idx)}


def reference(x, wc, wd, bias, offs):
    idx = offs[:16].T.reshape(-1)
    x, wc, wd, bias = f64(x), f64(wc), f64(wd), f64(bias)
    res = np.zeros((B, M, S))
    for a in range(B):
        piece = idx[a * K * S:(a + 1) * K * S]
        d = x[a][:, piece] + np.tile(-x[a], (1, K))
        centre = wc.T @ x[a] + bias
        edge = (wd.T @ d).reshape(M, K, S)
        res[a] = np.maximum(centre[:, None, :] + edge, 0.0).max(axis=1)
    return res

@@ -1,0 +1,105 @@
+import concourse.mybir as mybir
+
+F32, BF16, U16 = mybir.dt.float32, mybir.dt.bfloat16, mybir.dt.uint16
+ADD, MAX = mybir.AluOpType.add, mybir.AluOpType.max
+RELU = mybir.ActivationFunctionType.Relu
+
+P = 128
+GRAPHS, CHANNELS, NODES, NEIGHBOURS, OUTS = 2, 512, 1024, 4, 512
+CBLOCKS = CHANNELS // P
+OBLOCKS = OUTS // P
+BANK = 512
+HALVES = NODES // BANK
+SLOTS = GRAPHS * NEIGHBOURS
+
+FLOPS = 2 * GRAPHS * CHANNELS * OUTS * NODES * (NEIGHBOURS + 1)
+
+
+def tile_graphconv2d_b_kernel(tc, x, wc, wd, bias, offs, out):
+    nc = tc.nc
+    with (
+        tc.tile_pool(name="held", bufs=1) as held,
+        tc.tile_pool(name="diff", bufs=6) as diff_pool,
+        tc.tile_pool(name="diff_bf", bufs=3 * CBLOCKS) as diff_bf_pool,
+        tc.tile_pool(name="rows", bufs=2 * OBLOCKS) as rows_pool,
+        tc.psum_pool(name="psum", bufs=8) as psum,
+    ):
+        offsets = held.tile([P, SLOTS * NODES // 16], U16, name="offsets")
+        nc.sync.dma_start(offsets[:], offs)
+        x_f32 = [[held.tile([P, NODES], F32, name=f"x{a}_{c}") for c in range(CBLOCKS)] for a in range(GRAPHS)]
+        for a in range(GRAPHS):
+            for c in range(CBLOCKS):
+                nc.sync.dma_start(x_f32[a][c][:], x[a, c * P : (c + 1) * P, :])
+        wd_sb = held.tile([P, CBLOCKS, OUTS], BF16, name="wd_sb")
+        nc.scalar.dma_start(wd_sb[:], wd.rearrange("(c p) o -> p c o", p=P))
+        wc_sb = held.tile([P, CBLOCKS, OUTS], BF16, name="wc_sb")
+        nc.scalar.dma_start(wc_sb[:], wc.rearrange("(c p) o -> p c o", p=P))
+        bias_sb = held.tile([P, OBLOCKS], F32, name="bias_sb")
+        with nc.allow_non_contiguous_dma(reason="512 bias values, one to a partition and block"):
+            nc.scalar.dma_start(bias_sb[:], bias.rearrange("(b p) o -> p (b o)", p=P))
+
+        x_neg = [[held.tile([P, NODES], F32, name=f"neg{a}_{c}") for c in range(CBLOCKS)] for a in range(GRAPHS)]
+        x_bf = [[held.tile([P, NODES], BF16, name=f"xbf{a}_{c}") for c in range(CBLOCKS)] for a in range(GRAPHS)]
+
+        def product(weights, moving, o):
+            banks = [psum.tile([P, BANK], F32, name=f"bank{h}", tag="bank") for h in range(HALVES)]
+            for c in range(CBLOCKS):
+                for h in range(HALVES):
+                    nc.tensor.matmul(
+                        banks[h][:],
+                        weights[:, c, o * P : (o + 1) * P],
+                        moving[c][:, h * BANK : (h + 1) * BANK],
+                        start=(c == 0),
+                        stop=(c == CBLOCKS - 1),
+                    )
+            return banks
+
+        def prepare(a):
+            for c in range(CBLOCKS):
+                nc.scalar.mul(x_neg[a][c][:], x_f32[a][c][:], -1.0)
+            for c in range(CBLOCKS):
+                nc.scalar.copy(x_bf[a][c][:], x_f32[a][c][:])
+            centre = []
+            for o in range(OBLOCKS):
+                banks = product(wc_sb, x_bf[a], o)
+                row = rows_pool.tile([P, NODES], F32, name=f"centre{o}", tag="centre")
+                for h in range(HALVES):
+                    nc.scalar.copy(row[:, h * BANK : (h + 1) * BANK], banks[h][:])
+                centre.append(row)
+            return centre
+
+        def look_up(slot):
+            a = slot // NEIGHBOURS
+            piece = offsets[:, slot * (NODES // 16) : (slot + 1) * (NODES // 16)]
+            rounded = []
+            for c in range(CBLOCKS):
+                diff = diff_pool.tile([P, NODES], F32, name="diff")
+                nc.vector.tensor_tensor(diff[:], x_f32[a][c][:].indirect(piece), x_neg[a][c][:], ADD)
+                diff_bf = diff_bf_pool.tile([P, NODES], BF16, name="diff_bf")
+                nc.scalar.copy(diff_bf[:], diff[:])
+                rounded.append(diff_bf)
+            return rounded
+
+        centre = prepare(0)
+        rounded = look_up(0)
+        for slot in range(SLOTS):
+            a, r = divmod(slot, NEIGHBOURS)
+            this_centre, this_rounded = centre, rounded
+            if slot + 1 < SLOTS:
+                if r == NEIGHBOURS - 1:
+                    centre = prepare(a + 1)
+                rounded = look_up(slot + 1)
+            if r == 0:
+                best = [rows_pool.tile([P, NODES], F32, name=f"best{o}", tag="best") for o in range(OBLOCKS)]
+            for o in range(OBLOCKS):
+                banks = product(wd_sb, this_rounded, o)
+                for h in range(HALVES):
+                    half = best[o][:, h * BANK : (h + 1) * BANK]
+                    if r == 0:
+                        nc.scalar.copy(half, banks[h][:])
+                    else:
+                        nc.vector.tensor_tensor(half, banks[h][:], half, MAX)
+                if r == NEIGHBOURS - 1:
+                    nc.vector.tensor_tensor(best[o][:], best[o][:], this_centre[o][:], ADD)
+                    nc.scalar.activation(best[o][:], best[o][:], RELU, bias=bias_sb[:, o : o + 1])
+                    nc.sync.dma_start(out[a, o * P : (o + 1) * P, :], best[o][:])

@@ -19,21 +19,22 @@ def tile_graphconv2d_b_kernel(tc, x, wc, wd, bias, offs, out):
     nc = tc.nc
     with (
         tc.tile_pool(name="held", bufs=1) as held,
-        tc.tile_pool(name="diff", bufs=6) as diff_pool,
-        tc.tile_pool(name="diff_bf", bufs=3 * CBLOCKS) as diff_bf_pool,
+        tc.tile_pool(name="diff", bufs=4) as diff_pool,
+        tc.tile_pool(name="diff_bf", bufs=2 * CBLOCKS) as diff_bf_pool,
         tc.tile_pool(name="rows", bufs=2 * OBLOCKS) as rows_pool,
         tc.psum_pool(name="psum", bufs=8) as psum,
     ):
         offsets = held.tile([P, SLOTS * NODES // 16], U16, name="offsets")
         nc.sync.dma_start(offsets[:], offs)
         x_f32 = [[held.tile([P, NODES], F32, name=f"x{a}_{c}") for c in range(CBLOCKS)] for a in range(GRAPHS)]
+        wc_sb = held.tile([P, CBLOCKS, OUTS], BF16, name="wc_sb")
+        wd_sb = held.tile([P, CBLOCKS, OUTS], BF16, name="wd_sb")
         for a in range(GRAPHS):
             for c in range(CBLOCKS):
                 nc.sync.dma_start(x_f32[a][c][:], x[a, c * P : (c + 1) * P, :])
-        wd_sb = held.tile([P, CBLOCKS, OUTS], BF16, name="wd_sb")
-        nc.scalar.dma_start(wd_sb[:], wd.rearrange("(c p) o -> p c o", p=P))
-        wc_sb = held.tile([P, CBLOCKS, OUTS], BF16, name="wc_sb")
-        nc.scalar.dma_start(wc_sb[:], wc.rearrange("(c p) o -> p c o", p=P))
+            if a == 0:
+                nc.sync.dma_start(wc_sb[:], wc.rearrange("(c p) o -> p c o", p=P))
+                nc.sync.dma_start(wd_sb[:], wd.rearrange("(c p) o -> p c o", p=P))
         bias_sb = held.tile([P, OBLOCKS], F32, name="bias_sb")
         with nc.allow_non_contiguous_dma(reason="512 bias values, one to a partition and block"):
             nc.scalar.dma_start(bias_sb[:], bias.rearrange("(b p) o -> p (b o)", p=P))
@@ -94,12 +95,13 @@ def tile_graphconv2d_b_kernel(tc, x, wc, wd, bias, offs, out):
             for o in range(OBLOCKS):
                 banks = product(wd_sb, this_rounded, o)
                 for h in range(HALVES):
-                    half = best[o][:, h * BANK : (h + 1) * BANK]
+                    nodes = slice(h * BANK, (h + 1) * BANK)
+                    half = best[o][:, nodes]
                     if r == 0:
                         nc.scalar.copy(half, banks[h][:])
                     else:
                         nc.vector.tensor_tensor(half, banks[h][:], half, MAX)
-                if r == NEIGHBOURS - 1:
-                    nc.vector.tensor_tensor(best[o][:], best[o][:], this_centre[o][:], ADD)
-                    nc.scalar.activation(best[o][:], best[o][:], RELU, bias=bias_sb[:, o : o + 1])
-                    nc.sync.dma_start(out[a, o * P : (o + 1) * P, :], best[o][:])
+                    if r == NEIGHBOURS - 1:
+                        nc.vector.tensor_tensor(half, half, this_centre[o][:, nodes], ADD)
+                        nc.scalar.activation(half, half, RELU, bias=bias_sb[:, o : o + 1])
+                        nc.sync.dma_start(out[a, o * P : (o + 1) * P, nodes], half)

@@ -19,19 +19,20 @@ def tile_graphconv2d_b_kernel(tc, x, wc, wd, bias, offs, out):
     nc = tc.nc
     with (
         tc.tile_pool(name="held", bufs=1) as held,
-        tc.tile_pool(name="diff", bufs=4) as diff_pool,
-        tc.tile_pool(name="diff_bf", bufs=2 * CBLOCKS) as diff_bf_pool,
+        tc.tile_pool(name="diff", bufs=5) as diff_pool,
+        tc.tile_pool(name="diff_bf", bufs=6) as diff_bf_pool,
         tc.tile_pool(name="rows", bufs=2 * OBLOCKS) as rows_pool,
         tc.psum_pool(name="psum", bufs=8) as psum,
     ):
         offsets = held.tile([P, SLOTS * NODES // 16], U16, name="offsets")
-        nc.sync.dma_start(offsets[:], offs)
         x_f32 = [[held.tile([P, NODES], F32, name=f"x{a}_{c}") for c in range(CBLOCKS)] for a in range(GRAPHS)]
         wc_sb = held.tile([P, CBLOCKS, OUTS], BF16, name="wc_sb")
         wd_sb = held.tile([P, CBLOCKS, OUTS], BF16, name="wd_sb")
         for a in range(GRAPHS):
             for c in range(CBLOCKS):
                 nc.sync.dma_start(x_f32[a][c][:], x[a, c * P : (c + 1) * P, :])
+                if a == 0 and c == 0:
+                    nc.sync.dma_start(offsets[:], offs)
             if a == 0:
                 nc.sync.dma_start(wc_sb[:], wc.rearrange("(c p) o -> p c o", p=P))
                 nc.sync.dma_start(wd_sb[:], wd.rearrange("(c p) o -> p c o", p=P))
@@ -57,7 +58,10 @@ def tile_graphconv2d_b_kernel(tc, x, wc, wd, bias, offs, out):
 
         def prepare(a):
             for c in range(CBLOCKS):
-                nc.scalar.mul(x_neg[a][c][:], x_f32[a][c][:], -1.0)
+                if a == 0 and c == 0:
+                    nc.vector.tensor_scalar_mul(x_neg[a][c][:], x_f32[a][c][:], -1.0)
+                else:
+                    nc.scalar.mul(x_neg[a][c][:], x_f32[a][c][:], -1.0)
             for c in range(CBLOCKS):
                 nc.scalar.copy(x_bf[a][c][:], x_f32[a][c][:])
             centre = []

@@ -98,6 +98,12 @@ def tile_graphconv2d_b_kernel(tc, x, wc, wd, bias, offs, out):
                 best = [rows_pool.tile([P, NODES], F32, name=f"best{o}", tag="best") for o in range(OBLOCKS)]
             for o in range(OBLOCKS):
                 banks = product(wd_sb, this_rounded, o)
+                if 0 < r < NEIGHBOURS - 1:
+                    other = rows_pool.tile([P, NODES], F32, name=f"other{o}", tag="other")
+                    for h in range(HALVES):
+                        nc.scalar.copy(other[:, h * BANK : (h + 1) * BANK], banks[h][:])
+                    nc.vector.tensor_tensor(best[o][:], best[o][:], other[:], MAX)
+                    continue
                 for h in range(HALVES):
                     nodes = slice(h * BANK, (h + 1) * BANK)
                     half = best[o][:, nodes]

@@ -1,4 +1,5 @@
 import concourse.mybir as mybir
+from concourse.masks import make_identity
 
 F32, BF16, U16 = mybir.dt.float32, mybir.dt.bfloat16, mybir.dt.uint16
 ADD, MAX = mybir.AluOpType.add, mybir.AluOpType.max
@@ -11,6 +12,8 @@ OBLOCKS = OUTS // P
 BANK = 512
 HALVES = NODES // BANK
 SLOTS = GRAPHS * NEIGHBOURS
+PSUM_BANKS = 8
+JOINED = (1, 0)
 
 FLOPS = 2 * GRAPHS * CHANNELS * OUTS * NODES * (NEIGHBOURS + 1)
 
@@ -22,7 +25,8 @@ def tile_graphconv2d_b_kernel(tc, x, wc, wd, bias, offs, out):
         tc.tile_pool(name="diff", bufs=5) as diff_pool,
         tc.tile_pool(name="diff_bf", bufs=6) as diff_bf_pool,
         tc.tile_pool(name="rows", bufs=2 * OBLOCKS) as rows_pool,
-        tc.psum_pool(name="psum", bufs=8) as psum,
+        tc.psum_pool(name="psum", bufs=PSUM_BANKS - max(JOINED) * HALVES) as psum,
+        tc.psum_pool(name="psum_open", bufs=max(JOINED) * HALVES) as psum_open,
     ):
         offsets = held.tile([P, SLOTS * NODES // 16], U16, name="offsets")
         x_f32 = [[held.tile([P, NODES], F32, name=f"x{a}_{c}") for c in range(CBLOCKS)] for a in range(GRAPHS)]
@@ -40,11 +44,14 @@ def tile_graphconv2d_b_kernel(tc, x, wc, wd, bias, offs, out):
         with nc.allow_non_contiguous_dma(reason="512 bias values, one to a partition and block"):
             nc.scalar.dma_start(bias_sb[:], bias.rearrange("(b p) o -> p (b o)", p=P))
 
+        identity = held.tile([P, P], F32, name="identity")
+        make_identity(nc, identity[:])
+
         x_neg = [[held.tile([P, NODES], F32, name=f"neg{a}_{c}") for c in range(CBLOCKS)] for a in range(GRAPHS)]
         x_bf = [[held.tile([P, NODES], BF16, name=f"xbf{a}_{c}") for c in range(CBLOCKS)] for a in range(GRAPHS)]
 
-        def product(weights, moving, o):
-            banks = [psum.tile([P, BANK], F32, name=f"bank{h}", tag="bank") for h in range(HALVES)]
+        def product(weights, moving, o, pool=psum, close=True):
+            banks = [pool.tile([P, BANK], F32, name=f"bank{h}", tag="bank") for h in range(HALVES)]
             for c in range(CBLOCKS):
                 for h in range(HALVES):
                     nc.tensor.matmul(
@@ -52,7 +59,7 @@ def tile_graphconv2d_b_kernel(tc, x, wc, wd, bias, offs, out):
                         weights[:, c, o * P : (o + 1) * P],
                         moving[c][:, h * BANK : (h + 1) * BANK],
                         start=(c == 0),
-                        stop=(c == CBLOCKS - 1),
+                        stop=(close and c == CBLOCKS - 1),
                     )
             return banks
 
@@ -64,14 +71,26 @@ def tile_graphconv2d_b_kernel(tc, x, wc, wd, bias, offs, out):
                     nc.scalar.mul(x_neg[a][c][:], x_f32[a][c][:], -1.0)
             for c in range(CBLOCKS):
                 nc.scalar.copy(x_bf[a][c][:], x_f32[a][c][:])
-            centre = []
-            for o in range(OBLOCKS):
+            centre = [None] * JOINED[a]
+            for o in range(JOINED[a], OBLOCKS):
                 banks = product(wc_sb, x_bf[a], o)
                 row = rows_pool.tile([P, NODES], F32, name=f"centre{o}", tag="centre")
                 for h in range(HALVES):
                     nc.scalar.copy(row[:, h * BANK : (h + 1) * BANK], banks[h][:])
                 centre.append(row)
             return centre
+
+        def open_centre(a):
+            return [product(wc_sb, x_bf[a], o, pool=psum_open, close=False) for o in range(JOINED[a])]
+
+        def close_centre(a, groups, maxima):
+            for o in range(JOINED[a]):
+                for h in range(HALVES):
+                    nodes = slice(h * BANK, (h + 1) * BANK)
+                    half = maxima[o][:, nodes]
+                    nc.tensor.matmul(groups[o][h][:], identity[:], half, start=False, stop=True)
+                    nc.scalar.activation(half, groups[o][h][:], RELU, bias=bias_sb[:, o : o + 1])
+                    nc.sync.dma_start(out[a, o * P : (o + 1) * P, nodes], half)
 
         def look_up(slot):
             a = slot // NEIGHBOURS
@@ -86,7 +105,10 @@ def tile_graphconv2d_b_kernel(tc, x, wc, wd, bias, offs, out):
             return rounded
 
         centre = prepare(0)
+        groups = open_centre(0)
         rounded = look_up(0)
+        best = None
+        unfinished = []
         for slot in range(SLOTS):
             a, r = divmod(slot, NEIGHBOURS)
             this_centre, this_rounded = centre, rounded
@@ -95,6 +117,7 @@ def tile_graphconv2d_b_kernel(tc, x, wc, wd, bias, offs, out):
                     centre = prepare(a + 1)
                 rounded = look_up(slot + 1)
             if r == 0:
+                finished = best
                 best = [rows_pool.tile([P, NODES], F32, name=f"best{o}", tag="best") for o in range(OBLOCKS)]
             for o in range(OBLOCKS):
                 banks = product(wd_sb, this_rounded, o)
@@ -111,7 +134,16 @@ def tile_graphconv2d_b_kernel(tc, x, wc, wd, bias, offs, out):
                         nc.scalar.copy(half, banks[h][:])
                     else:
                         nc.vector.tensor_tensor(half, banks[h][:], half, MAX)
-                    if r == NEIGHBOURS - 1:
-                        nc.vector.tensor_tensor(half, half, this_centre[o][:, nodes], ADD)
-                        nc.scalar.activation(half, half, RELU, bias=bias_sb[:, o : o + 1])
-                        nc.sync.dma_start(out[a, o * P : (o + 1) * P, nodes], half)
+                    if r == NEIGHBOURS - 1 and o >= JOINED[a]:
+                        adder = nc.gpsimd if slot == SLOTS - 1 and h == HALVES - 1 else nc.vector
+                        adder.tensor_tensor(half, half, this_centre[o][:, nodes], ADD)
+                        unfinished.append((a, o, nodes, half))
+            if r != NEIGHBOURS - 1 or slot == SLOTS - 1:
+                for a_done, o, nodes, half in unfinished:
+                    nc.scalar.activation(half, half, RELU, bias=bias_sb[:, o : o + 1])
+                    nc.sync.dma_start(out[a_done, o * P : (o + 1) * P, nodes], half)
+                unfinished.clear()
+            if r == 0 and a > 0:
+                close_centre(a - 1, groups, finished)
+                groups = open_centre(a)
+        close_centre(GRAPHS - 1, groups, best)

@@ -135,7 +135,7 @@ def tile_graphconv2d_b_kernel(tc, x, wc, wd, bias, offs, out):
                     else:
                         nc.vector.tensor_tensor(half, banks[h][:], half, MAX)
                     if r == NEIGHBOURS - 1 and o >= JOINED[a]:
-                        adder = nc.gpsimd if slot == SLOTS - 1 and h == HALVES - 1 else nc.vector
+                        adder = nc.gpsimd if slot == SLOTS - 1 and h == HALVES - 1 and o < OBLOCKS - 1 else nc.vector
                         adder.tensor_tensor(half, half, this_centre[o][:, nodes], ADD)
                         unfinished.append((a, o, nodes, half))
             if r != NEIGHBOURS - 1 or slot == SLOTS - 1:

@@ -128,13 +128,15 @@ def tile_graphconv2d_b_kernel(tc, x, wc, wd, bias, offs, out):
                     nc.vector.tensor_tensor(best[o][:], best[o][:], other[:], MAX)
                     continue
                 for h in range(HALVES):
-                    nodes = slice(h * BANK, (h + 1) * BANK)
-                    half = best[o][:, nodes]
+                    half = best[o][:, h * BANK : (h + 1) * BANK]
                     if r == 0:
                         nc.scalar.copy(half, banks[h][:])
                     else:
                         nc.vector.tensor_tensor(half, banks[h][:], half, MAX)
-                    if r == NEIGHBOURS - 1 and o >= JOINED[a]:
+                if r == NEIGHBOURS - 1 and o >= JOINED[a]:
+                    for h in range(HALVES):
+                        nodes = slice(h * BANK, (h + 1) * BANK)
+                        half = best[o][:, nodes]
                         adder = nc.gpsimd if slot == SLOTS - 1 and h == HALVES - 1 and o < OBLOCKS - 1 else nc.vector
                         adder.tensor_tensor(half, half, this_centre[o][:, nodes], ADD)
                         unfinished.append((a, o, nodes, half))

@@ -14,6 +14,9 @@ HALVES = NODES // BANK
 SLOTS = GRAPHS * NEIGHBOURS
 PSUM_BANKS = 8
 JOINED = (1, 0)
+VECTOR_ROWS = 14
+SCALAR_ROWS = 22
+SIDE_NEG, SIDE_XBF, SIDE_CENTRE, SIDE_CLOSE, SIDE_FINISH = 2, 3, 4, 5, 7
 
 FLOPS = 2 * GRAPHS * CHANNELS * OUTS * NODES * (NEIGHBOURS + 1)
 
@@ -22,9 +25,8 @@ def tile_graphconv2d_b_kernel(tc, x, wc, wd, bias, offs, out):
     nc = tc.nc
     with (
         tc.tile_pool(name="held", bufs=1) as held,
-        tc.tile_pool(name="diff", bufs=5) as diff_pool,
-        tc.tile_pool(name="diff_bf", bufs=6) as diff_bf_pool,
-        tc.tile_pool(name="rows", bufs=2 * OBLOCKS) as rows_pool,
+        tc.tile_pool(name="vector_rows", bufs=VECTOR_ROWS) as vector_rows,
+        tc.tile_pool(name="scalar_rows", bufs=SCALAR_ROWS) as scalar_rows,
         tc.psum_pool(name="psum", bufs=PSUM_BANKS - max(JOINED) * HALVES) as psum,
         tc.psum_pool(name="psum_open", bufs=max(JOINED) * HALVES) as psum_open,
     ):
@@ -43,12 +45,19 @@ def tile_graphconv2d_b_kernel(tc, x, wc, wd, bias, offs, out):
         bias_sb = held.tile([P, OBLOCKS], F32, name="bias_sb")
         with nc.allow_non_contiguous_dma(reason="512 bias values, one to a partition and block"):
             nc.scalar.dma_start(bias_sb[:], bias.rearrange("(b p) o -> p (b o)", p=P))
-
         identity = held.tile([P, P], F32, name="identity")
         make_identity(nc, identity[:])
-
         x_neg = [[held.tile([P, NODES], F32, name=f"neg{a}_{c}") for c in range(CBLOCKS)] for a in range(GRAPHS)]
         x_bf = [[held.tile([P, NODES], BF16, name=f"xbf{a}_{c}") for c in range(CBLOCKS)] for a in range(GRAPHS)]
+
+        def vector_row(name):
+            return vector_rows.tile([P, NODES], F32, name=name, tag="vector_row")
+
+        def scalar_row(name, dtype=F32):
+            return scalar_rows.tile([P, NODES], dtype, name=name, tag="scalar_row")
+
+        def halves(row):
+            return [row[:, h * BANK : (h + 1) * BANK] for h in range(HALVES)]
 
         def product(weights, moving, o, pool=psum, close=True):
             banks = [pool.tile([P, BANK], F32, name=f"bank{h}", tag="bank") for h in range(HALVES)]
@@ -63,89 +72,104 @@ def tile_graphconv2d_b_kernel(tc, x, wc, wd, bias, offs, out):
                     )
             return banks
 
-        def prepare(a):
-            for c in range(CBLOCKS):
-                if a == 0 and c == 0:
-                    nc.vector.tensor_scalar_mul(x_neg[a][c][:], x_f32[a][c][:], -1.0)
-                else:
-                    nc.scalar.mul(x_neg[a][c][:], x_f32[a][c][:], -1.0)
-            for c in range(CBLOCKS):
-                nc.scalar.copy(x_bf[a][c][:], x_f32[a][c][:])
-            centre = [None] * JOINED[a]
-            for o in range(JOINED[a], OBLOCKS):
-                banks = product(wc_sb, x_bf[a], o)
-                row = rows_pool.tile([P, NODES], F32, name=f"centre{o}", tag="centre")
-                for h in range(HALVES):
-                    nc.scalar.copy(row[:, h * BANK : (h + 1) * BANK], banks[h][:])
-                centre.append(row)
-            return centre
+        def copy_out(banks, name):
+            row = scalar_row(name)
+            for half, bank in zip(halves(row), banks):
+                nc.scalar.copy(half, bank[:])
+            return row
 
-        def open_centre(a):
-            return [product(wc_sb, x_bf[a], o, pool=psum_open, close=False) for o in range(JOINED[a])]
+        def negate(a, c):
+            if a == 0 and c == 0:
+                nc.vector.tensor_scalar_mul(x_neg[a][c][:], x_f32[a][c][:], -1.0)
+            else:
+                nc.scalar.mul(x_neg[a][c][:], x_f32[a][c][:], -1.0)
 
-        def close_centre(a, groups, maxima):
-            for o in range(JOINED[a]):
-                for h in range(HALVES):
-                    nodes = slice(h * BANK, (h + 1) * BANK)
-                    half = maxima[o][:, nodes]
-                    nc.tensor.matmul(groups[o][h][:], identity[:], half, start=False, stop=True)
-                    nc.scalar.activation(half, groups[o][h][:], RELU, bias=bias_sb[:, o : o + 1])
-                    nc.sync.dma_start(out[a, o * P : (o + 1) * P, nodes], half)
+        def round_x(a, c):
+            nc.scalar.copy(x_bf[a][c][:], x_f32[a][c][:])
 
-        def look_up(slot):
+        def look_up(slot, c):
             a = slot // NEIGHBOURS
             piece = offsets[:, slot * (NODES // 16) : (slot + 1) * (NODES // 16)]
-            rounded = []
-            for c in range(CBLOCKS):
-                diff = diff_pool.tile([P, NODES], F32, name="diff")
-                nc.vector.tensor_tensor(diff[:], x_f32[a][c][:].indirect(piece), x_neg[a][c][:], ADD)
-                diff_bf = diff_bf_pool.tile([P, NODES], BF16, name="diff_bf")
-                nc.scalar.copy(diff_bf[:], diff[:])
-                rounded.append(diff_bf)
-            return rounded
+            diff = vector_row("diff")
+            nc.vector.tensor_tensor(diff[:], x_f32[a][c][:].indirect(piece), x_neg[a][c][:], ADD)
+            diff_bf = scalar_row("diff_bf", BF16)
+            nc.scalar.copy(diff_bf[:], diff[:])
+            return diff_bf
 
-        centre = prepare(0)
-        groups = open_centre(0)
-        rounded = look_up(0)
-        best = None
-        unfinished = []
+        def finish(a, o, sources, row):
+            for h in range(HALVES):
+                half = halves(row)[h]
+                nc.scalar.activation(half, sources[h], RELU, bias=bias_sb[:, o : o + 1])
+                nc.sync.dma_start(out[a, o * P : (o + 1) * P, h * BANK : (h + 1) * BANK], half)
+
+        def close(a, groups, best):
+            for o in range(JOINED[a]):
+                for h in range(HALVES):
+                    nc.tensor.matmul(groups[o][h][:], identity[:], halves(best[o])[h], start=False, stop=True)
+                finish(a, o, [bank[:] for bank in groups[o]], best[o])
+
+        for c in range(CBLOCKS):
+            negate(0, c)
+        rounded = []
+        for c in range(CBLOCKS):
+            rounded.append(look_up(0, c))
+            round_x(0, c)
+        groups = [product(wc_sb, x_bf[0], o, pool=psum_open, close=False) for o in range(JOINED[0])]
+        centre = [None] * JOINED[0] + [copy_out(product(wc_sb, x_bf[0], o), f"centre{o}") for o in range(JOINED[0], OBLOCKS)]
+
+        def merge(slot, o, best, other, centre):
+            last = slot == SLOTS - 1
+            merged = vector_row(f"best{o}")
+            if last:
+                for h in range(HALVES):
+                    nc.vector.tensor_tensor(halves(merged)[h], other[h][:], halves(best[o])[h], MAX)
+            else:
+                nc.vector.tensor_tensor(merged[:], best[o][:], other[:], MAX)
+            best[o] = merged
+            if slot % NEIGHBOURS == NEIGHBOURS - 1 and o >= JOINED[slot // NEIGHBOURS]:
+                for h in range(HALVES):
+                    adder = nc.gpsimd if last and h == HALVES - 1 and o < OBLOCKS - 1 else nc.vector
+                    adder.tensor_tensor(halves(merged)[h], halves(merged)[h], halves(centre[o])[h], ADD)
+
+        side = []
+        best, rows = None, None
         for slot in range(SLOTS):
             a, r = divmod(slot, NEIGHBOURS)
-            this_centre, this_rounded = centre, rounded
-            if slot + 1 < SLOTS:
-                if r == NEIGHBOURS - 1:
-                    centre = prepare(a + 1)
-                rounded = look_up(slot + 1)
-            if r == 0:
-                finished = best
-                best = [rows_pool.tile([P, NODES], F32, name=f"best{o}", tag="best") for o in range(OBLOCKS)]
-            for o in range(OBLOCKS):
-                banks = product(wd_sb, this_rounded, o)
-                if 0 < r < NEIGHBOURS - 1:
-                    other = rows_pool.tile([P, NODES], F32, name=f"other{o}", tag="other")
-                    for h in range(HALVES):
-                        nc.scalar.copy(other[:, h * BANK : (h + 1) * BANK], banks[h][:])
-                    nc.vector.tensor_tensor(best[o][:], best[o][:], other[:], MAX)
-                    continue
-                for h in range(HALVES):
-                    half = best[o][:, h * BANK : (h + 1) * BANK]
-                    if r == 0:
-                        nc.scalar.copy(half, banks[h][:])
+            last = slot == SLOTS - 1
+            if slot == SIDE_NEG:
+                side.extend([lambda c=c: negate(1, c) for c in range(CBLOCKS)])
+            if slot == SIDE_XBF:
+                side.extend([lambda c=c: round_x(1, c) for c in range(CBLOCKS)])
+            if slot == SIDE_CENTRE:
+                next_centre = [None] * OBLOCKS
+                def centre_job(o):
+                    next_centre[o] = copy_out(product(wc_sb, x_bf[1], o), f"centre{o}")
+                side.extend([lambda o=o: centre_job(o) for o in range(JOINED[1], OBLOCKS)])
+            upcoming, new_rows = [], []
+            for k in range(CBLOCKS):
+                if not last:
+                    upcoming.append(look_up(slot + 1, k))
+                banks = product(wd_sb, rounded, k)
+                new_rows.append(banks if last else copy_out(banks, f"edge{k}"))
+                if slot > 0:
+                    if (slot - 1) % NEIGHBOURS == 0:
+                        if k == 0:
+                            best = rows
                     else:
-                        nc.vector.tensor_tensor(half, banks[h][:], half, MAX)
-                if r == NEIGHBOURS - 1 and o >= JOINED[a]:
-                    for h in range(HALVES):
-                        nodes = slice(h * BANK, (h + 1) * BANK)
-                        half = best[o][:, nodes]
-                        adder = nc.gpsimd if slot == SLOTS - 1 and h == HALVES - 1 and o < OBLOCKS - 1 else nc.vector
-                        adder.tensor_tensor(half, half, this_centre[o][:, nodes], ADD)
-                        unfinished.append((a, o, nodes, half))
-            if r != NEIGHBOURS - 1 or slot == SLOTS - 1:
-                for a_done, o, nodes, half in unfinished:
-                    nc.scalar.activation(half, half, RELU, bias=bias_sb[:, o : o + 1])
-                    nc.sync.dma_start(out[a_done, o * P : (o + 1) * P, nodes], half)
-                unfinished.clear()
-            if r == 0 and a > 0:
-                close_centre(a - 1, groups, finished)
-                groups = open_centre(a)
-        close_centre(GRAPHS - 1, groups, best)
+                        merge(slot - 1, k, best, rows[k], centre)
+                if side:
+                    side.pop(0)()
+            if slot == NEIGHBOURS:
+                done, centre = best, next_centre
+            if slot == SIDE_CLOSE:
+                close(0, groups, done)
+                groups = [product(wc_sb, x_bf[1], o, pool=psum_open, close=False) for o in range(JOINED[1])]
+            if slot == SIDE_FINISH:
+                for o in range(JOINED[0], OBLOCKS):
+                    finish(0, o, halves(done[o]), done[o])
+            rounded, rows = upcoming, new_rows
+        for o in range(OBLOCKS):
+            merge(SLOTS - 1, o, best, rows[o], centre)
+        for o in range(JOINED[1], OBLOCKS):
+            finish(1, o, halves(best[o]), best[o])
+        close(1, groups, best)

@@ -4,6 +4,7 @@ from concourse.masks import make_identity
 F32, BF16, U16 = mybir.dt.float32, mybir.dt.bfloat16, mybir.dt.uint16
 ADD, MAX = mybir.AluOpType.add, mybir.AluOpType.max
 RELU = mybir.ActivationFunctionType.Relu
+IDENTITY = mybir.ActivationFunctionType.Identity
 
 P = 128
 GRAPHS, CHANNELS, NODES, NEIGHBOURS, OUTS = 2, 512, 1024, 4, 512
@@ -13,10 +14,16 @@ BANK = 512
 HALVES = NODES // BANK
 SLOTS = GRAPHS * NEIGHBOURS
 PSUM_BANKS = 8
-JOINED = (1, 0)
+JOINED = (0, 0)
 VECTOR_ROWS = 14
 SCALAR_ROWS = 22
-SIDE_NEG, SIDE_XBF, SIDE_CENTRE, SIDE_CLOSE, SIDE_FINISH = 2, 3, 4, 5, 7
+WC_AFTER, WD_AFTER = 3, 3
+HELD = 2
+DIRECT = (6,)
+TAIL_ADDS = True
+LATE = ()
+LATE_AT = ()
+SIDE_NEG, SIDE_XBF, SIDE_CENTRE, SIDE_CLOSE, SIDE_FINISH = 1, 2, 3, 9, 7
 
 FLOPS = 2 * GRAPHS * CHANNELS * OUTS * NODES * (NEIGHBOURS + 1)
 
@@ -28,7 +35,7 @@ def tile_graphconv2d_b_kernel(tc, x, wc, wd, bias, offs, out):
         tc.tile_pool(name="vector_rows", bufs=VECTOR_ROWS) as vector_rows,
         tc.tile_pool(name="scalar_rows", bufs=SCALAR_ROWS) as scalar_rows,
         tc.psum_pool(name="psum", bufs=PSUM_BANKS - max(JOINED) * HALVES) as psum,
-        tc.psum_pool(name="psum_open", bufs=max(JOINED) * HALVES) as psum_open,
+        tc.psum_pool(name="psum_open", bufs=max(max(JOINED) * HALVES, 1)) as psum_open,
     ):
         offsets = held.tile([P, SLOTS * NODES // 16], U16, name="offsets")
         x_f32 = [[held.tile([P, NODES], F32, name=f"x{a}_{c}") for c in range(CBLOCKS)] for a in range(GRAPHS)]
@@ -39,9 +46,10 @@ def tile_graphconv2d_b_kernel(tc, x, wc, wd, bias, offs, out):
                 nc.sync.dma_start(x_f32[a][c][:], x[a, c * P : (c + 1) * P, :])
                 if a == 0 and c == 0:
                     nc.sync.dma_start(offsets[:], offs)
-            if a == 0:
-                nc.sync.dma_start(wc_sb[:], wc.rearrange("(c p) o -> p c o", p=P))
-                nc.sync.dma_start(wd_sb[:], wd.rearrange("(c p) o -> p c o", p=P))
+                if a == 0 and c == WC_AFTER:
+                    nc.sync.dma_start(wc_sb[:], wc.rearrange("(c p) o -> p c o", p=P))
+                if a == 0 and c == WD_AFTER:
+                    nc.sync.dma_start(wd_sb[:], wd.rearrange("(c p) o -> p c o", p=P))
         bias_sb = held.tile([P, OBLOCKS], F32, name="bias_sb")
         with nc.allow_non_contiguous_dma(reason="512 bias values, one to a partition and block"):
             nc.scalar.dma_start(bias_sb[:], bias.rearrange("(b p) o -> p (b o)", p=P))
@@ -114,19 +122,19 @@ def tile_graphconv2d_b_kernel(tc, x, wc, wd, bias, offs, out):
         for c in range(CBLOCKS):
             rounded.append(look_up(0, c))
             round_x(0, c)
-        groups = [product(wc_sb, x_bf[0], o, pool=psum_open, close=False) for o in range(JOINED[0])]
-        centre = [None] * JOINED[0] + [copy_out(product(wc_sb, x_bf[0], o), f"centre{o}") for o in range(JOINED[0], OBLOCKS)]
+        groups = [product(wc_sb, x_bf[0], o, close=False) for o in range(HELD)]
+        centre = [None if o < HELD or o in LATE else copy_out(product(wc_sb, x_bf[0], o), f"centre{o}") for o in range(OBLOCKS)]
 
         def merge(slot, o, best, other, centre):
             last = slot == SLOTS - 1
             merged = vector_row(f"best{o}")
-            if last:
+            if last or slot in DIRECT:
                 for h in range(HALVES):
                     nc.vector.tensor_tensor(halves(merged)[h], other[h][:], halves(best[o])[h], MAX)
             else:
                 nc.vector.tensor_tensor(merged[:], best[o][:], other[:], MAX)
             best[o] = merged
-            if slot % NEIGHBOURS == NEIGHBOURS - 1 and o >= JOINED[slot // NEIGHBOURS]:
+            if slot % NEIGHBOURS == NEIGHBOURS - 1 and o >= JOINED[slot // NEIGHBOURS] and not (slot < NEIGHBOURS and (o in LATE or o < HELD or TAIL_ADDS)):
                 for h in range(HALVES):
                     adder = nc.gpsimd if last and h == HALVES - 1 and o < OBLOCKS - 1 else nc.vector
                     adder.tensor_tensor(halves(merged)[h], halves(merged)[h], halves(centre[o])[h], ADD)
@@ -150,23 +158,45 @@ def tile_graphconv2d_b_kernel(tc, x, wc, wd, bias, offs, out):
                 if not last:
                     upcoming.append(look_up(slot + 1, k))
                 banks = product(wd_sb, rounded, k)
-                new_rows.append(banks if last else copy_out(banks, f"edge{k}"))
+                new_rows.append(banks if last or slot in DIRECT else copy_out(banks, f"edge{k}"))
                 if slot > 0:
                     if (slot - 1) % NEIGHBOURS == 0:
                         if k == 0:
                             best = rows
-                    else:
+                    elif not (slot == NEIGHBOURS and k < HELD):
                         merge(slot - 1, k, best, rows[k], centre)
+                if slot == NEIGHBOURS - 1 and k >= CBLOCKS - HELD:
+                    merge(slot, k - (CBLOCKS - HELD), best, new_rows[k - (CBLOCKS - HELD)], centre)
                 if side:
                     side.pop(0)()
+            if slot == NEIGHBOURS - 1:
+                for o in range(HELD):
+                    for h in range(HALVES):
+                        nc.tensor.matmul(groups[o][h][:], identity[:], halves(best[o])[h], start=False, stop=True)
+                    finish(0, o, [bank[:] for bank in groups[o]], best[o])
             if slot == NEIGHBOURS:
-                done, centre = best, next_centre
+                done, old_centre, centre = best, centre, next_centre
             if slot == SIDE_CLOSE:
                 close(0, groups, done)
                 groups = [product(wc_sb, x_bf[1], o, pool=psum_open, close=False) for o in range(JOINED[1])]
+            for o in LATE:
+                if LATE_AT[LATE.index(o)] == slot:
+                    group = product(wc_sb, x_bf[0], o, close=False)
+                    for h in range(HALVES):
+                        nc.tensor.matmul(group[h][:], identity[:], halves(done[o])[h], start=False, stop=True)
+                    finish(0, o, [bank[:] for bank in group], done[o])
             if slot == SIDE_FINISH:
-                for o in range(JOINED[0], OBLOCKS):
-                    finish(0, o, halves(done[o]), done[o])
+                for o in range(HELD, OBLOCKS):
+                    if o not in LATE:
+                        if TAIL_ADDS:
+                            shifted = scalar_row(f"shifted{o}")
+                            nc.scalar.activation(shifted[:], old_centre[o][:], IDENTITY, bias=bias_sb[:, o : o + 1])
+                            for h in range(HALVES):
+                                nc.gpsimd.tensor_tensor(halves(done[o])[h], halves(done[o])[h], halves(shifted)[h], ADD)
+                                nc.scalar.activation(halves(done[o])[h], halves(done[o])[h], RELU)
+                                nc.sync.dma_start(out[0, o * P : (o + 1) * P, h * BANK : (h + 1) * BANK], halves(done[o])[h])
+                        else:
+                            finish(0, o, halves(done[o]), done[o])
             rounded, rows = upcoming, new_rows
         for o in range(OBLOCKS):
             merge(SLOTS - 1, o, best, rows[o], centre)

@@ -18,12 +18,15 @@ JOINED = (0, 0)
 VECTOR_ROWS = 14
 SCALAR_ROWS = 22
 WC_AFTER, WD_AFTER = 3, 3
+C0_AT = -1
+STEPPED = (2,)
+LAG = 1
 HELD = 2
 DIRECT = (6,)
 TAIL_ADDS = True
 LATE = ()
 LATE_AT = ()
-SIDE_NEG, SIDE_XBF, SIDE_CENTRE, SIDE_CLOSE, SIDE_FINISH = 1, 2, 3, 9, 7
+SIDE_START, SIDE_ORDER, SIDE_PER_STEP, SIDE_CLOSE, SIDE_FINISH = 1, "nnnnxxxxcccc", (1, 1, 1, 1, 1, 1, 1, 1), 9, 7
 
 FLOPS = 2 * GRAPHS * CHANNELS * OUTS * NODES * (NEIGHBOURS + 1)
 
@@ -123,12 +126,12 @@ def tile_graphconv2d_b_kernel(tc, x, wc, wd, bias, offs, out):
             rounded.append(look_up(0, c))
             round_x(0, c)
         groups = [product(wc_sb, x_bf[0], o, close=False) for o in range(HELD)]
-        centre = [None if o < HELD or o in LATE else copy_out(product(wc_sb, x_bf[0], o), f"centre{o}") for o in range(OBLOCKS)]
+        centre = [None if o < HELD or o in LATE or C0_AT >= 0 else copy_out(product(wc_sb, x_bf[0], o), f"centre{o}") for o in range(OBLOCKS)]
 
         def merge(slot, o, best, other, centre):
             last = slot == SLOTS - 1
             merged = vector_row(f"best{o}")
-            if last or slot in DIRECT:
+            if last or slot in DIRECT or slot in STEPPED:
                 for h in range(HALVES):
                     nc.vector.tensor_tensor(halves(merged)[h], other[h][:], halves(best[o])[h], MAX)
             else:
@@ -141,34 +144,44 @@ def tile_graphconv2d_b_kernel(tc, x, wc, wd, bias, offs, out):
 
         side = []
         best, rows = None, None
+        waiting, step = [], 0
         for slot in range(SLOTS):
             a, r = divmod(slot, NEIGHBOURS)
             last = slot == SLOTS - 1
-            if slot == SIDE_NEG:
-                side.extend([lambda c=c: negate(1, c) for c in range(CBLOCKS)])
-            if slot == SIDE_XBF:
-                side.extend([lambda c=c: round_x(1, c) for c in range(CBLOCKS)])
-            if slot == SIDE_CENTRE:
+            if slot == SIDE_START:
                 next_centre = [None] * OBLOCKS
                 def centre_job(o):
                     next_centre[o] = copy_out(product(wc_sb, x_bf[1], o), f"centre{o}")
-                side.extend([lambda o=o: centre_job(o) for o in range(JOINED[1], OBLOCKS)])
+                jobs = {"n": [lambda c=c: negate(1, c) for c in range(CBLOCKS)], "x": [lambda c=c: round_x(1, c) for c in range(CBLOCKS)], "c": [lambda o=o: centre_job(o) for o in range(JOINED[1], OBLOCKS)]}
+                for kind in SIDE_ORDER:
+                    side.append(jobs[kind].pop(0))
+            if slot == C0_AT:
+                def old_centre_job(o):
+                    old_centre[o] = copy_out(product(wc_sb, x_bf[0], o), f"centre{o}")
+                side.extend([lambda o=o: old_centre_job(o) for o in range(HELD, OBLOCKS)])
             upcoming, new_rows = [], []
             for k in range(CBLOCKS):
                 if not last:
                     upcoming.append(look_up(slot + 1, k))
                 banks = product(wd_sb, rounded, k)
-                new_rows.append(banks if last or slot in DIRECT else copy_out(banks, f"edge{k}"))
+                new_rows.append(banks if last or slot in DIRECT or slot in STEPPED else copy_out(banks, f"edge{k}"))
+                if slot in STEPPED:
+                    waiting.append((step, slot, k, banks))
                 if slot > 0:
                     if (slot - 1) % NEIGHBOURS == 0:
                         if k == 0:
                             best = rows
-                    elif not (slot == NEIGHBOURS and k < HELD):
+                    elif not (slot == NEIGHBOURS and k < HELD) and (slot - 1) not in STEPPED:
                         merge(slot - 1, k, best, rows[k], centre)
+                while waiting and step - waiting[0][0] >= LAG:
+                    made, s, o, held_banks = waiting.pop(0)
+                    merge(s, o, best, held_banks, centre)
+                step += 1
                 if slot == NEIGHBOURS - 1 and k >= CBLOCKS - HELD:
                     merge(slot, k - (CBLOCKS - HELD), best, new_rows[k - (CBLOCKS - HELD)], centre)
-                if side:
-                    side.pop(0)()
+                for unused in range(SIDE_PER_STEP[slot]):
+                    if side:
+                        side.pop(0)()
             if slot == NEIGHBOURS - 1:
                 for o in range(HELD):
                     for h in range(HALVES):

@@ -131,7 +131,7 @@ def tile_graphconv2d_b_kernel(tc, x, wc, wd, bias, offs, out):
         def merge(slot, o, best, other, centre):
             last = slot == SLOTS - 1
             merged = vector_row(f"best{o}")
-            if last or slot in DIRECT or slot in STEPPED:
+            if last or (slot in DIRECT and o > 0) or slot in STEPPED:
                 for h in range(HALVES):
                     nc.vector.tensor_tensor(halves(merged)[h], other[h][:], halves(best[o])[h], MAX)
             else:
@@ -164,7 +164,7 @@ def tile_graphconv2d_b_kernel(tc, x, wc, wd, bias, offs, out):
                 if not last:
                     upcoming.append(look_up(slot + 1, k))
                 banks = product(wd_sb, rounded, k)
-                new_rows.append(banks if last or slot in DIRECT or slot in STEPPED else copy_out(banks, f"edge{k}"))
+                new_rows.append(banks if last or (slot in DIRECT and k > 0) or slot in STEPPED else copy_out(banks, f"edge{k}"))
                 if slot in STEPPED:
                     waiting.append((step, slot, k, banks))
                 if slot > 0:

@@ -8,25 +8,15 @@ IDENTITY = mybir.ActivationFunctionType.Identity
 
 P = 128
 GRAPHS, CHANNELS, NODES, NEIGHBOURS, OUTS = 2, 512, 1024, 4, 512
-CBLOCKS = CHANNELS // P
-OBLOCKS = OUTS // P
+BLOCKS = CHANNELS // P
 BANK = 512
 HALVES = NODES // BANK
 SLOTS = GRAPHS * NEIGHBOURS
+LIST_COLUMNS = NODES // 16
 PSUM_BANKS = 8
-JOINED = (0, 0)
+HELD = 2
 VECTOR_ROWS = 14
 SCALAR_ROWS = 22
-WC_AFTER, WD_AFTER = 3, 3
-C0_AT = -1
-STEPPED = (2,)
-LAG = 1
-HELD = 2
-DIRECT = (6,)
-TAIL_ADDS = True
-LATE = ()
-LATE_AT = ()
-SIDE_START, SIDE_ORDER, SIDE_PER_STEP, SIDE_CLOSE, SIDE_FINISH = 1, "nnnnxxxxcccc", (1, 1, 1, 1, 1, 1, 1, 1), 9, 7
 
 FLOPS = 2 * GRAPHS * CHANNELS * OUTS * NODES * (NEIGHBOURS + 1)
 
@@ -37,29 +27,27 @@ def tile_graphconv2d_b_kernel(tc, x, wc, wd, bias, offs, out):
         tc.tile_pool(name="held", bufs=1) as held,
         tc.tile_pool(name="vector_rows", bufs=VECTOR_ROWS) as vector_rows,
         tc.tile_pool(name="scalar_rows", bufs=SCALAR_ROWS) as scalar_rows,
-        tc.psum_pool(name="psum", bufs=PSUM_BANKS - max(JOINED) * HALVES) as psum,
-        tc.psum_pool(name="psum_open", bufs=max(max(JOINED) * HALVES, 1)) as psum_open,
+        tc.psum_pool(name="psum", bufs=PSUM_BANKS) as psum,
     ):
-        offsets = held.tile([P, SLOTS * NODES // 16], U16, name="offsets")
-        x_f32 = [[held.tile([P, NODES], F32, name=f"x{a}_{c}") for c in range(CBLOCKS)] for a in range(GRAPHS)]
-        wc_sb = held.tile([P, CBLOCKS, OUTS], BF16, name="wc_sb")
-        wd_sb = held.tile([P, CBLOCKS, OUTS], BF16, name="wd_sb")
-        for a in range(GRAPHS):
-            for c in range(CBLOCKS):
-                nc.sync.dma_start(x_f32[a][c][:], x[a, c * P : (c + 1) * P, :])
-                if a == 0 and c == 0:
-                    nc.sync.dma_start(offsets[:], offs)
-                if a == 0 and c == WC_AFTER:
-                    nc.sync.dma_start(wc_sb[:], wc.rearrange("(c p) o -> p c o", p=P))
-                if a == 0 and c == WD_AFTER:
-                    nc.sync.dma_start(wd_sb[:], wd.rearrange("(c p) o -> p c o", p=P))
-        bias_sb = held.tile([P, OBLOCKS], F32, name="bias_sb")
+        offsets = held.tile([P, SLOTS * LIST_COLUMNS], U16, name="offsets")
+        x_f32 = [[held.tile([P, NODES], F32, name=f"x{a}_{c}") for c in range(BLOCKS)] for a in range(GRAPHS)]
+        wc_sb = held.tile([P, BLOCKS, OUTS], BF16, name="wc_sb")
+        wd_sb = held.tile([P, BLOCKS, OUTS], BF16, name="wd_sb")
+        nc.sync.dma_start(x_f32[0][0][:], x[0, 0:P, :])
+        nc.sync.dma_start(offsets[:], offs)
+        for c in range(1, BLOCKS):
+            nc.sync.dma_start(x_f32[0][c][:], x[0, c * P : (c + 1) * P, :])
+        nc.sync.dma_start(wc_sb[:], wc.rearrange("(c p) o -> p c o", p=P))
+        nc.sync.dma_start(wd_sb[:], wd.rearrange("(c p) o -> p c o", p=P))
+        for c in range(BLOCKS):
+            nc.sync.dma_start(x_f32[1][c][:], x[1, c * P : (c + 1) * P, :])
+        bias_sb = held.tile([P, BLOCKS], F32, name="bias_sb")
         with nc.allow_non_contiguous_dma(reason="512 bias values, one to a partition and block"):
             nc.scalar.dma_start(bias_sb[:], bias.rearrange("(b p) o -> p (b o)", p=P))
         identity = held.tile([P, P], F32, name="identity")
         make_identity(nc, identity[:])
-        x_neg = [[held.tile([P, NODES], F32, name=f"neg{a}_{c}") for c in range(CBLOCKS)] for a in range(GRAPHS)]
-        x_bf = [[held.tile([P, NODES], BF16, name=f"xbf{a}_{c}") for c in range(CBLOCKS)] for a in range(GRAPHS)]
+        x_neg = [[held.tile([P, NODES], F32, name=f"neg{a}_{c}") for c in range(BLOCKS)] for a in range(GRAPHS)]
+        x_bf = [[held.tile([P, NODES], BF16, name=f"xbf{a}_{c}") for c in range(BLOCKS)] for a in range(GRAPHS)]
 
         def vector_row(name):
             return vector_rows.tile([P, NODES], F32, name=name, tag="vector_row")
@@ -70,16 +58,16 @@ def tile_graphconv2d_b_kernel(tc, x, wc, wd, bias, offs, out):
         def halves(row):
             return [row[:, h * BANK : (h + 1) * BANK] for h in range(HALVES)]
 
-        def product(weights, moving, o, pool=psum, close=True):
-            banks = [pool.tile([P, BANK], F32, name=f"bank{h}", tag="bank") for h in range(HALVES)]
-            for c in range(CBLOCKS):
+        def product(weights, moving, o, close=True):
+            banks = [psum.tile([P, BANK], F32, name=f"bank{h}", tag="bank") for h in range(HALVES)]
+            for c in range(BLOCKS):
                 for h in range(HALVES):
                     nc.tensor.matmul(
                         banks[h][:],
                         weights[:, c, o * P : (o + 1) * P],
                         moving[c][:, h * BANK : (h + 1) * BANK],
                         start=(c == 0),
-                        stop=(close and c == CBLOCKS - 1),
+                        stop=(close and c == BLOCKS - 1),
                     )
             return banks
 
@@ -90,129 +78,97 @@ def tile_graphconv2d_b_kernel(tc, x, wc, wd, bias, offs, out):
             return row
 
         def negate(a, c):
-            if a == 0 and c == 0:
-                nc.vector.tensor_scalar_mul(x_neg[a][c][:], x_f32[a][c][:], -1.0)
-            else:
-                nc.scalar.mul(x_neg[a][c][:], x_f32[a][c][:], -1.0)
+            nc.scalar.mul(x_neg[a][c][:], x_f32[a][c][:], -1.0)
 
         def round_x(a, c):
             nc.scalar.copy(x_bf[a][c][:], x_f32[a][c][:])
 
         def look_up(slot, c):
             a = slot // NEIGHBOURS
-            piece = offsets[:, slot * (NODES // 16) : (slot + 1) * (NODES // 16)]
+            piece = offsets[:, slot * LIST_COLUMNS : (slot + 1) * LIST_COLUMNS]
             diff = vector_row("diff")
             nc.vector.tensor_tensor(diff[:], x_f32[a][c][:].indirect(piece), x_neg[a][c][:], ADD)
             diff_bf = scalar_row("diff_bf", BF16)
             nc.scalar.copy(diff_bf[:], diff[:])
             return diff_bf
 
-        def finish(a, o, sources, row):
-            for h in range(HALVES):
-                half = halves(row)[h]
-                nc.scalar.activation(half, sources[h], RELU, bias=bias_sb[:, o : o + 1])
-                nc.sync.dma_start(out[a, o * P : (o + 1) * P, h * BANK : (h + 1) * BANK], half)
-
-        def close(a, groups, best):
-            for o in range(JOINED[a]):
+        def merge(best, edge, o):
+            merged = vector_row(f"best{o}")
+            if isinstance(edge[o], list):
                 for h in range(HALVES):
-                    nc.tensor.matmul(groups[o][h][:], identity[:], halves(best[o])[h], start=False, stop=True)
-                finish(a, o, [bank[:] for bank in groups[o]], best[o])
+                    nc.vector.tensor_tensor(halves(merged)[h], edge[o][h][:], halves(best[o])[h], MAX)
+            else:
+                nc.vector.tensor_tensor(merged[:], best[o][:], edge[o][:], MAX)
+            best[o] = merged
 
-        for c in range(CBLOCKS):
+        def relu_and_store(a, o, h, source, row, with_bias):
+            half = halves(row)[h]
+            if with_bias:
+                nc.scalar.activation(half, source, RELU, bias=bias_sb[:, o : o + 1])
+            else:
+                nc.scalar.activation(half, source, RELU)
+            nc.sync.dma_start(out[a, o * P : (o + 1) * P, h * BANK : (h + 1) * BANK], half)
+
+        nc.vector.tensor_scalar_mul(x_neg[0][0][:], x_f32[0][0][:], -1.0)
+        for c in range(1, BLOCKS):
             negate(0, c)
         rounded = []
-        for c in range(CBLOCKS):
+        for c in range(BLOCKS):
             rounded.append(look_up(0, c))
             round_x(0, c)
-        groups = [product(wc_sb, x_bf[0], o, close=False) for o in range(HELD)]
-        centre = [None if o < HELD or o in LATE or C0_AT >= 0 else copy_out(product(wc_sb, x_bf[0], o), f"centre{o}") for o in range(OBLOCKS)]
+        open_centre = [product(wc_sb, x_bf[0], o, close=False) for o in range(HELD)]
+        centre = [[None] * BLOCKS for a in range(GRAPHS)]
+        for o in range(HELD, BLOCKS):
+            centre[0][o] = copy_out(product(wc_sb, x_bf[0], o), f"centre{o}")
 
-        def merge(slot, o, best, other, centre):
-            last = slot == SLOTS - 1
-            merged = vector_row(f"best{o}")
-            if last or (slot in DIRECT and o > 0) or slot in STEPPED:
-                for h in range(HALVES):
-                    nc.vector.tensor_tensor(halves(merged)[h], other[h][:], halves(best[o])[h], MAX)
-            else:
-                nc.vector.tensor_tensor(merged[:], best[o][:], other[:], MAX)
-            best[o] = merged
-            if slot % NEIGHBOURS == NEIGHBOURS - 1 and o >= JOINED[slot // NEIGHBOURS] and not (slot < NEIGHBOURS and (o in LATE or o < HELD or TAIL_ADDS)):
-                for h in range(HALVES):
-                    adder = nc.gpsimd if last and h == HALVES - 1 and o < OBLOCKS - 1 else nc.vector
-                    adder.tensor_tensor(halves(merged)[h], halves(merged)[h], halves(centre[o])[h], ADD)
-
-        side = []
-        best, rows = None, None
-        waiting, step = [], 0
+        best = [None] * GRAPHS
+        edges = [None] * SLOTS
         for slot in range(SLOTS):
             a, r = divmod(slot, NEIGHBOURS)
-            last = slot == SLOTS - 1
-            if slot == SIDE_START:
-                next_centre = [None] * OBLOCKS
-                def centre_job(o):
-                    next_centre[o] = copy_out(product(wc_sb, x_bf[1], o), f"centre{o}")
-                jobs = {"n": [lambda c=c: negate(1, c) for c in range(CBLOCKS)], "x": [lambda c=c: round_x(1, c) for c in range(CBLOCKS)], "c": [lambda o=o: centre_job(o) for o in range(JOINED[1], OBLOCKS)]}
-                for kind in SIDE_ORDER:
-                    side.append(jobs[kind].pop(0))
-            if slot == C0_AT:
-                def old_centre_job(o):
-                    old_centre[o] = copy_out(product(wc_sb, x_bf[0], o), f"centre{o}")
-                side.extend([lambda o=o: old_centre_job(o) for o in range(HELD, OBLOCKS)])
-            upcoming, new_rows = [], []
-            for k in range(CBLOCKS):
-                if not last:
-                    upcoming.append(look_up(slot + 1, k))
+            edges[slot] = []
+            coming = []
+            for k in range(BLOCKS):
+                if slot + 1 < SLOTS:
+                    coming.append(look_up(slot + 1, k))
                 banks = product(wd_sb, rounded, k)
-                new_rows.append(banks if last or (slot in DIRECT and k > 0) or slot in STEPPED else copy_out(banks, f"edge{k}"))
-                if slot in STEPPED:
-                    waiting.append((step, slot, k, banks))
-                if slot > 0:
-                    if (slot - 1) % NEIGHBOURS == 0:
-                        if k == 0:
-                            best = rows
-                    elif not (slot == NEIGHBOURS and k < HELD) and (slot - 1) not in STEPPED:
-                        merge(slot - 1, k, best, rows[k], centre)
-                while waiting and step - waiting[0][0] >= LAG:
-                    made, s, o, held_banks = waiting.pop(0)
-                    merge(s, o, best, held_banks, centre)
-                step += 1
-                if slot == NEIGHBOURS - 1 and k >= CBLOCKS - HELD:
-                    merge(slot, k - (CBLOCKS - HELD), best, new_rows[k - (CBLOCKS - HELD)], centre)
-                for unused in range(SIDE_PER_STEP[slot]):
-                    if side:
-                        side.pop(0)()
-            if slot == NEIGHBOURS - 1:
+                stays = slot == 2 or (slot == 6 and k > 0) or slot == 7
+                edges[slot].append(banks if stays else copy_out(banks, f"edge{k}"))
+                if slot in (1, 5) and k == 0:
+                    best[a] = edges[slot - 1]
+                if slot in (2, 6, 7) or (slot == 4 and k >= HELD):
+                    merge(best[(slot - 1) // NEIGHBOURS], edges[slot - 1], k)
+                if slot == 2 and k >= 1:
+                    merge(best[0], edges[2], k - 1)
+                if slot == 3 and k == 0:
+                    merge(best[0], edges[2], BLOCKS - 1)
+                if slot == 3 and k >= BLOCKS - HELD:
+                    merge(best[0], edges[3], k - (BLOCKS - HELD))
+                if slot == 1:
+                    round_x(1, k)
+                if slot == 2:
+                    centre[1][k] = copy_out(product(wc_sb, x_bf[1], k), f"centre{k}")
+                    negate(1, k)
+            if slot == 3:
                 for o in range(HELD):
                     for h in range(HALVES):
-                        nc.tensor.matmul(groups[o][h][:], identity[:], halves(best[o])[h], start=False, stop=True)
-                    finish(0, o, [bank[:] for bank in groups[o]], best[o])
-            if slot == NEIGHBOURS:
-                done, old_centre, centre = best, centre, next_centre
-            if slot == SIDE_CLOSE:
-                close(0, groups, done)
-                groups = [product(wc_sb, x_bf[1], o, pool=psum_open, close=False) for o in range(JOINED[1])]
-            for o in LATE:
-                if LATE_AT[LATE.index(o)] == slot:
-                    group = product(wc_sb, x_bf[0], o, close=False)
+                        nc.tensor.matmul(open_centre[o][h][:], identity[:], halves(best[0][o])[h], start=False, stop=True)
                     for h in range(HALVES):
-                        nc.tensor.matmul(group[h][:], identity[:], halves(done[o])[h], start=False, stop=True)
-                    finish(0, o, [bank[:] for bank in group], done[o])
-            if slot == SIDE_FINISH:
-                for o in range(HELD, OBLOCKS):
-                    if o not in LATE:
-                        if TAIL_ADDS:
-                            shifted = scalar_row(f"shifted{o}")
-                            nc.scalar.activation(shifted[:], old_centre[o][:], IDENTITY, bias=bias_sb[:, o : o + 1])
-                            for h in range(HALVES):
-                                nc.gpsimd.tensor_tensor(halves(done[o])[h], halves(done[o])[h], halves(shifted)[h], ADD)
-                                nc.scalar.activation(halves(done[o])[h], halves(done[o])[h], RELU)
-                                nc.sync.dma_start(out[0, o * P : (o + 1) * P, h * BANK : (h + 1) * BANK], halves(done[o])[h])
-                        else:
-                            finish(0, o, halves(done[o]), done[o])
-            rounded, rows = upcoming, new_rows
-        for o in range(OBLOCKS):
-            merge(SLOTS - 1, o, best, rows[o], centre)
-        for o in range(JOINED[1], OBLOCKS):
-            finish(1, o, halves(best[o]), best[o])
-        close(1, groups, best)
+                        relu_and_store(0, o, h, open_centre[o][h][:], best[0][o], with_bias=True)
+            rounded = coming
+
+        for o in range(HELD, BLOCKS):
+            shifted = scalar_row(f"shifted{o}")
+            nc.scalar.activation(shifted[:], centre[0][o][:], IDENTITY, bias=bias_sb[:, o : o + 1])
+            for h in range(HALVES):
+                half = halves(best[0][o])[h]
+                nc.gpsimd.tensor_tensor(half, half, halves(shifted)[h], ADD)
+                relu_and_store(0, o, h, half, best[0][o], with_bias=False)
+        for o in range(BLOCKS):
+            merge(best[1], edges[SLOTS - 1], o)
+            for h in range(HALVES):
+                adder = nc.gpsimd if h == HALVES - 1 and o < BLOCKS - 1 else nc.vector
+                half = halves(best[1][o])[h]
+                adder.tensor_tensor(half, half, halves(centre[1][o])[h], ADD)
+        for o in range(BLOCKS):
+            for h in range(HALVES):
+                relu_and_store(1, o, h, halves(best[1][o])[h], best[1][o], with_bias=True)

@@ -118,8 +118,7 @@ def tile_graphconv2d_b_kernel(tc, x, wc, wd, bias, offs, out):
             round_x(0, c)
         open_centre = [product(wc_sb, x_bf[0], o, close=False) for o in range(HELD)]
         centre = [[None] * BLOCKS for a in range(GRAPHS)]
-        for o in range(HELD, BLOCKS):
-            centre[0][o] = copy_out(product(wc_sb, x_bf[0], o), f"centre{o}")
+        centres_to_come = [(0, o) for o in range(HELD, BLOCKS)] + [(1, o) for o in range(BLOCKS)]
 
         best = [None] * GRAPHS
         edges = [None] * SLOTS
@@ -146,8 +145,10 @@ def tile_graphconv2d_b_kernel(tc, x, wc, wd, bias, offs, out):
                 if slot == 1:
                     round_x(1, k)
                 if slot == 2:
-                    centre[1][k] = copy_out(product(wc_sb, x_bf[1], k), f"centre{k}")
                     negate(1, k)
+                if slot == 2 or (slot == 4 and k >= HELD):
+                    graph, o = centres_to_come.pop(0)
+                    centre[graph][o] = copy_out(product(wc_sb, x_bf[graph], o), f"centre{o}")
             if slot == 3:
                 for o in range(HELD):
                     for h in range(HALVES):

@@ -15,6 +15,7 @@ SLOTS = GRAPHS * NEIGHBOURS
 LIST_COLUMNS = NODES // 16
 PSUM_BANKS = 8
 HELD = 2
+LATE = 2
 VECTOR_ROWS = 14
 SCALAR_ROWS = 22
 
@@ -118,7 +119,13 @@ def tile_graphconv2d_b_kernel(tc, x, wc, wd, bias, offs, out):
             round_x(0, c)
         open_centre = [product(wc_sb, x_bf[0], o, close=False) for o in range(HELD)]
         centre = [[None] * BLOCKS for a in range(GRAPHS)]
-        centres_to_come = [(0, o) for o in range(HELD, BLOCKS)] + [(1, o) for o in range(BLOCKS)]
+        centres_to_come = [(0, o) for o in range(LATE + 1, BLOCKS)] + [(1, o) for o in range(BLOCKS)]
+
+        def join(o, group):
+            for h in range(HALVES):
+                nc.tensor.matmul(group[h][:], identity[:], halves(best[0][o])[h], start=False, stop=True)
+            for h in range(HALVES):
+                relu_and_store(0, o, h, group[h][:], best[0][o], with_bias=True)
 
         best = [None] * GRAPHS
         edges = [None] * SLOTS
@@ -146,18 +153,17 @@ def tile_graphconv2d_b_kernel(tc, x, wc, wd, bias, offs, out):
                     round_x(1, k)
                 if slot == 2:
                     negate(1, k)
-                if slot == 2 or (slot == 4 and k >= HELD):
+                if slot == 2 or (slot == 4 and k == BLOCKS - 1):
                     graph, o = centres_to_come.pop(0)
                     centre[graph][o] = copy_out(product(wc_sb, x_bf[graph], o), f"centre{o}")
             if slot == 3:
                 for o in range(HELD):
-                    for h in range(HALVES):
-                        nc.tensor.matmul(open_centre[o][h][:], identity[:], halves(best[0][o])[h], start=False, stop=True)
-                    for h in range(HALVES):
-                        relu_and_store(0, o, h, open_centre[o][h][:], best[0][o], with_bias=True)
+                    join(o, open_centre[o])
+            if slot == 4:
+                join(LATE, product(wc_sb, x_bf[0], LATE, close=False))
             rounded = coming
 
-        for o in range(HELD, BLOCKS):
+        for o in range(LATE + 1, BLOCKS):
             shifted = scalar_row(f"shifted{o}")
             nc.scalar.activation(shifted[:], centre[0][o][:], IDENTITY, bias=bias_sb[:, o : o + 1])
             for h in range(HALVES):

@@ -119,7 +119,8 @@ def tile_graphconv2d_b_kernel(tc, x, wc, wd, bias, offs, out):
             round_x(0, c)
         open_centre = [product(wc_sb, x_bf[0], o, close=False) for o in range(HELD)]
         centre = [[None] * BLOCKS for a in range(GRAPHS)]
-        centres_to_come = [(0, o) for o in range(LATE + 1, BLOCKS)] + [(1, o) for o in range(BLOCKS)]
+        for o in range(LATE + 1, BLOCKS):
+            centre[0][o] = copy_out(product(wc_sb, x_bf[0], o), f"centre{o}")
 
         def join(o, group):
             for h in range(HALVES):
@@ -153,9 +154,8 @@ def tile_graphconv2d_b_kernel(tc, x, wc, wd, bias, offs, out):
                     round_x(1, k)
                 if slot == 2:
                     negate(1, k)
-                if slot == 2 or (slot == 4 and k == BLOCKS - 1):
-                    graph, o = centres_to_come.pop(0)
-                    centre[graph][o] = copy_out(product(wc_sb, x_bf[graph], o), f"centre{o}")
+                if slot == 2:
+                    centre[1][k] = copy_out(product(wc_sb, x_bf[1], k), f"centre{k}")
             if slot == 3:
                 for o in range(HELD):
                     join(o, open_centre[o])

@@ -178,4 +178,9 @@ def tile_graphconv2d_b_kernel(tc, x, wc, wd, bias, offs, out):
                 adder.tensor_tensor(half, half, halves(centre[1][o])[h], ADD)
         for o in range(BLOCKS):
             for h in range(HALVES):
-                relu_and_store(1, o, h, halves(best[1][o])[h], best[1][o], with_bias=True)
+                if (o, h) != (BLOCKS - 1, HALVES - 1):
+                    relu_and_store(1, o, h, halves(best[1][o])[h], best[1][o], with_bias=True)
+        o, h = BLOCKS - 1, HALVES - 1
+        half = halves(best[1][o])[h]
+        nc.vector.tensor_scalar(half, half, bias_sb[:, o : o + 1], 0.0, ADD, MAX)
+        nc.sync.dma_start(out[1, o * P : (o + 1) * P, h * BANK : (h + 1) * BANK], half)

import concourse.mybir as mybir
from concourse.masks import make_identity

F32, BF16, U16 = mybir.dt.float32, mybir.dt.bfloat16, mybir.dt.uint16
ADD, MAX = mybir.AluOpType.add, mybir.AluOpType.max
RELU = mybir.ActivationFunctionType.Relu
IDENTITY = mybir.ActivationFunctionType.Identity

P = 128
GRAPHS, CHANNELS, NODES, NEIGHBOURS, OUTS = 2, 512, 1024, 4, 512
BLOCKS = CHANNELS // P
BANK = 512
HALVES = NODES // BANK
SLOTS = GRAPHS * NEIGHBOURS
LIST_COLUMNS = NODES // 16
PSUM_BANKS = 8
HELD = 2
LATE = 2
VECTOR_ROWS = 14
SCALAR_ROWS = 22

FLOPS = 2 * GRAPHS * CHANNELS * OUTS * NODES * (NEIGHBOURS + 1)


def tile_graphconv2d_b_kernel(tc, x, wc, wd, bias, offs, out):
    nc = tc.nc
    with (
        tc.tile_pool(name="held", bufs=1) as held,
        tc.tile_pool(name="vector_rows", bufs=VECTOR_ROWS) as vector_rows,
        tc.tile_pool(name="scalar_rows", bufs=SCALAR_ROWS) as scalar_rows,
        tc.psum_pool(name="psum", bufs=PSUM_BANKS) as psum,
    ):
        offsets = held.tile([P, SLOTS * LIST_COLUMNS], U16, name="offsets")
        x_f32 = [[held.tile([P, NODES], F32, name=f"x{a}_{c}") for c in range(BLOCKS)] for a in range(GRAPHS)]
        wc_sb = held.tile([P, BLOCKS, OUTS], BF16, name="wc_sb")
        wd_sb = held.tile([P, BLOCKS, OUTS], BF16, name="wd_sb")
        nc.sync.dma_start(x_f32[0][0][:], x[0, 0:P, :])
        nc.sync.dma_start(offsets[:], offs)
        for c in range(1, BLOCKS):
            nc.sync.dma_start(x_f32[0][c][:], x[0, c * P : (c + 1) * P, :])
        nc.sync.dma_start(wc_sb[:], wc.rearrange("(c p) o -> p c o", p=P))
        nc.sync.dma_start(wd_sb[:], wd.rearrange("(c p) o -> p c o", p=P))
        for c in range(BLOCKS):
            nc.sync.dma_start(x_f32[1][c][:], x[1, c * P : (c + 1) * P, :])
        bias_sb = held.tile([P, BLOCKS], F32, name="bias_sb")
        with nc.allow_non_contiguous_dma(reason="512 bias values, one to a partition and block"):
            nc.scalar.dma_start(bias_sb[:], bias.rearrange("(b p) o -> p (b o)", p=P))
        identity = held.tile([P, P], F32, name="identity")
        make_identity(nc, identity[:])
        x_neg = [[held.tile([P, NODES], F32, name=f"neg{a}_{c}") for c in range(BLOCKS)] for a in range(GRAPHS)]
        x_bf = [[held.tile([P, NODES], BF16, name=f"xbf{a}_{c}") for c in range(BLOCKS)] for a in range(GRAPHS)]

        def vector_row(name):
            return vector_rows.tile([P, NODES], F32, name=name, tag="vector_row")

        def scalar_row(name, dtype=F32):
            return scalar_rows.tile([P, NODES], dtype, name=name, tag="scalar_row")

        def halves(row):
            return [row[:, h * BANK : (h + 1) * BANK] for h in range(HALVES)]

        def product(weights, moving, o, close=True):
            banks = [psum.tile([P, BANK], F32, name=f"bank{h}", tag="bank") for h in range(HALVES)]
            for c in range(BLOCKS):
                for h in range(HALVES):
                    nc.tensor.matmul(
                        banks[h][:],
                        weights[:, c, o * P : (o + 1) * P],
                        moving[c][:, h * BANK : (h + 1) * BANK],
                        start=(c == 0),
                        stop=(close and c == BLOCKS - 1),
                    )
            return banks

        def copy_out(banks, name):
            row = scalar_row(name)
            for half, bank in zip(halves(row), banks):
                nc.scalar.copy(half, bank[:])
            return row

        def negate(a, c):
            nc.scalar.mul(x_neg[a][c][:], x_f32[a][c][:], -1.0)

        def round_x(a, c):
            nc.scalar.copy(x_bf[a][c][:], x_f32[a][c][:])

        def look_up(slot, c):
            a = slot // NEIGHBOURS
            piece = offsets[:, slot * LIST_COLUMNS : (slot + 1) * LIST_COLUMNS]
            diff = vector_row("diff")
            nc.vector.tensor_tensor(diff[:], x_f32[a][c][:].indirect(piece), x_neg[a][c][:], ADD)
            diff_bf = scalar_row("diff_bf", BF16)
            nc.scalar.copy(diff_bf[:], diff[:])
            return diff_bf

        def merge(best, edge, o):
            merged = vector_row(f"best{o}")
            if isinstance(edge[o], list):
                for h in range(HALVES):
                    nc.vector.tensor_tensor(halves(merged)[h], edge[o][h][:], halves(best[o])[h], MAX)
            else:
                nc.vector.tensor_tensor(merged[:], best[o][:], edge[o][:], MAX)
            best[o] = merged

        def relu_and_store(a, o, h, source, row, with_bias):
            half = halves(row)[h]
            if with_bias:
                nc.scalar.activation(half, source, RELU, bias=bias_sb[:, o : o + 1])
            else:
                nc.scalar.activation(half, source, RELU)
            nc.sync.dma_start(out[a, o * P : (o + 1) * P, h * BANK : (h + 1) * BANK], half)

        nc.vector.tensor_scalar_mul(x_neg[0][0][:], x_f32[0][0][:], -1.0)
        for c in range(1, BLOCKS):
            negate(0, c)
        rounded = []
        for c in range(BLOCKS):
            rounded.append(look_up(0, c))
            round_x(0, c)
        open_centre = [product(wc_sb, x_bf[0], o, close=False) for o in range(HELD)]
        centre = [[None] * BLOCKS for a in range(GRAPHS)]
        for o in range(LATE + 1, BLOCKS):
            centre[0][o] = copy_out(product(wc_sb, x_bf[0], o), f"centre{o}")

        def join(o, group):
            for h in range(HALVES):
                nc.tensor.matmul(group[h][:], identity[:], halves(best[0][o])[h], start=False, stop=True)
            for h in range(HALVES):
                relu_and_store(0, o, h, group[h][:], best[0][o], with_bias=True)

        best = [None] * GRAPHS
        edges = [None] * SLOTS
        for slot in range(SLOTS):
            a, r = divmod(slot, NEIGHBOURS)
            edges[slot] = []
            coming = []
            for k in range(BLOCKS):
                if slot + 1 < SLOTS:
                    coming.append(look_up(slot + 1, k))
                banks = product(wd_sb, rounded, k)
                stays = slot == 2 or (slot == 6 and k > 0) or slot == 7
                edges[slot].append(banks if stays else copy_out(banks, f"edge{k}"))
                if slot in (1, 5) and k == 0:
                    best[a] = edges[slot - 1]
                if slot in (2, 6, 7) or (slot == 4 and k >= HELD):
                    merge(best[(slot - 1) // NEIGHBOURS], edges[slot - 1], k)
                if slot == 2 and k >= 1:
                    merge(best[0], edges[2], k - 1)
                if slot == 3 and k == 0:
                    merge(best[0], edges[2], BLOCKS - 1)
                if slot == 3 and k >= BLOCKS - HELD:
                    merge(best[0], edges[3], k - (BLOCKS - HELD))
                if slot == 1:
                    round_x(1, k)
                if slot == 2:
                    negate(1, k)
                if slot == 2:
                    centre[1][k] = copy_out(product(wc_sb, x_bf[1], k), f"centre{k}")
            if slot == 3:
                for o in range(HELD):
                    join(o, open_centre[o])
            if slot == 4:
                join(LATE, product(wc_sb, x_bf[0], LATE, close=False))
            rounded = coming

        for o in range(LATE + 1, BLOCKS):
            shifted = scalar_row(f"shifted{o}")
            nc.scalar.activation(shifted[:], centre[0][o][:], IDENTITY, bias=bias_sb[:, o : o + 1])
            for h in range(HALVES):
                half = halves(best[0][o])[h]
                nc.gpsimd.tensor_tensor(half, half, halves(shifted)[h], ADD)
                relu_and_store(0, o, h, half, best[0][o], with_bias=False)
        for o in range(BLOCKS):
            merge(best[1], edges[SLOTS - 1], o)
            for h in range(HALVES):
                adder = nc.gpsimd if h == HALVES - 1 and o < BLOCKS - 1 else nc.vector
                half = halves(best[1][o])[h]
                adder.tensor_tensor(half, half, halves(centre[1][o])[h], ADD)
        for o in range(BLOCKS):
            for h in range(HALVES):
                if (o, h) != (BLOCKS - 1, HALVES - 1):
                    relu_and_store(1, o, h, halves(best[1][o])[h], best[1][o], with_bias=True)
        o, h = BLOCKS - 1, HALVES - 1
        half = halves(best[1][o])[h]
        nc.vector.tensor_scalar(half, half, bias_sb[:, o : o + 1], 0.0, ADD, MAX)
        nc.sync.dma_start(out[1, o * P : (o + 1) * P, h * BANK : (h + 1) * BANK], half)
